import numpy as np
import ml_dtypes

BF16 = ml_dtypes.bfloat16


def bf(x):
    return np.asarray(x, np.float32).astype(BF16)


def f32(x):
    return np.asarray(x, np.float32)


def f64(x):
    return np.asarray(x).astype(np.float64)


def striped(idx):
    return np.tile(idx.reshape(-1, 16).T, (8, 1))


C, S, B, T, N = 256, 1024, 32, 64, 2048


def setup_inputs():
    return {"table": f32(0.5 * np.random.standard_normal((C, S))), "offs": striped(np.random.permutation(np.tile(np.arange(S), 2))[:N])}


def reference(table, offs):
    idx = offs[:16].T.reshape(-1)
    e = f64(table)[:, idx].reshape(C, B, T)
    return np.tanh(e[:, :, :-1] + e[:, :, 1:]).sum(axis=2)

@@ -1,0 +1,53 @@
+import concourse.mybir as mybir
+
+F32 = mybir.dt.float32
+U16 = mybir.dt.uint16
+COPY = mybir.ActivationFunctionType.Copy
+TANH = mybir.ActivationFunctionType.Tanh
+ADD = mybir.AluOpType.add
+INNERMOST = mybir.AxisListType.X
+
+P = 128
+FEATURES, VOCAB = 256, 1024
+SENTENCES, WORDS = 32, 64
+PAIRS = WORDS - 1
+LIST = SENTENCES * WORDS
+PIECE = VOCAB
+PIECE_SENTENCES = PIECE // WORDS
+OFFSETS_PER_COLUMN = 16
+
+
+def tile_bilingual_kernel(tc, table, offs, out):
+    nc = tc.nc
+    with tc.tile_pool(name="held", bufs=1) as held, tc.tile_pool(name="work", bufs=2) as work:
+        offsets = held.tile([P, LIST // OFFSETS_PER_COLUMN], U16, name="offsets")
+        nc.sync.dma_start(offsets[:], offs)
+
+        for block in range(FEATURES // P):
+            rows = slice(block * P, (block + 1) * P)
+            window = held.tile([P, VOCAB], F32, name=f"window{block}")
+            nc.sync.dma_start(window[:], table[rows, :])
+            sentence_sums = held.tile([P, SENTENCES], F32, name=f"sentence_sums{block}")
+
+            for piece in range(LIST // PIECE):
+                columns = slice(
+                    piece * PIECE // OFFSETS_PER_COLUMN, (piece + 1) * PIECE // OFFSETS_PER_COLUMN
+                )
+                picked = work.tile([P, PIECE], F32, name="picked")
+                nc.scalar.activation(picked[:], window[:].indirect(offsets[:, columns]), COPY)
+
+                words = picked[:].rearrange("p (b t) -> p b t", t=WORDS)
+                pair_sums = work.tile([P, PIECE_SENTENCES, PAIRS], F32, name="pair_sums")
+                nc.vector.tensor_tensor(
+                    pair_sums[:], words[:, :, 0:PAIRS], words[:, :, 1:WORDS], ADD
+                )
+
+                pair_tanh = work.tile([P, PIECE_SENTENCES, PAIRS], F32, name="pair_tanh")
+                nc.scalar.activation(pair_tanh[:], pair_sums[:], TANH)
+
+                first = piece * PIECE_SENTENCES
+                nc.vector.tensor_reduce(
+                    sentence_sums[:, first : first + PIECE_SENTENCES], pair_tanh[:], INNERMOST, ADD
+                )
+
+            nc.sync.dma_start(out[rows, :], sentence_sums[:])

@@ -23,6 +23,10 @@ def tile_bilingual_kernel(tc, table, offs, out):
         offsets = held.tile([P, LIST // OFFSETS_PER_COLUMN], U16, name="offsets")
         nc.sync.dma_start(offsets[:], offs)
 
+        dummy = held.tile([P, 1], F32, name="dummy")
+        nc.vector.memset(dummy[:], 0.0)
+        nc.scalar.activation(dummy[:], dummy[:], TANH)
+
         for block in range(FEATURES // P):
             rows = slice(block * P, (block + 1) * P)
             window = held.tile([P, VOCAB], F32, name=f"window{block}")

@@ -9,49 +9,65 @@ INNERMOST = mybir.AxisListType.X
 
 P = 128
 FEATURES, VOCAB = 256, 1024
+BLOCKS = FEATURES // P
 SENTENCES, WORDS = 32, 64
 PAIRS = WORDS - 1
 LIST = SENTENCES * WORDS
-PIECE = VOCAB
-PIECE_SENTENCES = PIECE // WORDS
 OFFSETS_PER_COLUMN = 16
+
+WIDTHS = (VOCAB, VOCAB)
+WIDTHS_OF_LAST_BLOCK = (VOCAB, VOCAB // 2, VOCAB // 4, VOCAB // 4)
+assert sum(WIDTHS) == LIST and sum(WIDTHS_OF_LAST_BLOCK) == LIST
+
+
+def cut_into_pieces():
+    pieces = []
+    for block in range(BLOCKS):
+        first = 0
+        for width in WIDTHS_OF_LAST_BLOCK if block == BLOCKS - 1 else WIDTHS:
+            pieces.append((block, first, width))
+            first += width
+    return pieces
 
 
 def tile_bilingual_kernel(tc, table, offs, out):
     nc = tc.nc
-    with tc.tile_pool(name="held", bufs=1) as held, tc.tile_pool(name="work", bufs=2) as work:
+    with tc.tile_pool(name="held", bufs=1) as held:
         offsets = held.tile([P, LIST // OFFSETS_PER_COLUMN], U16, name="offsets")
         nc.sync.dma_start(offsets[:], offs)
+        windows = [held.tile([P, VOCAB], F32, name=f"window{block}") for block in range(BLOCKS)]
+        for block in range(BLOCKS):
+            nc.sync.dma_start(windows[block][:], table[block * P : (block + 1) * P, :])
+        sentence_sums = [
+            held.tile([P, SENTENCES], F32, name=f"sentence_sums{block}") for block in range(BLOCKS)
+        ]
 
         dummy = held.tile([P, 1], F32, name="dummy")
         nc.vector.memset(dummy[:], 0.0)
         nc.scalar.activation(dummy[:], dummy[:], TANH)
 
-        for block in range(FEATURES // P):
-            rows = slice(block * P, (block + 1) * P)
-            window = held.tile([P, VOCAB], F32, name=f"window{block}")
-            nc.sync.dma_start(window[:], table[rows, :])
-            sentence_sums = held.tile([P, SENTENCES], F32, name=f"sentence_sums{block}")
+        def look_up_and_add(k, block, first, width):
+            columns = slice(first // OFFSETS_PER_COLUMN, (first + width) // OFFSETS_PER_COLUMN)
+            picked = held.tile([P, width], F32, name=f"picked{k}")
+            nc.scalar.activation(picked[:], windows[block][:].indirect(offsets[:, columns]), COPY)
+            words = picked[:].rearrange("p (b t) -> p b t", t=WORDS)
+            pair_sums = held.tile([P, width // WORDS, PAIRS], F32, name=f"pair_sums{k}")
+            nc.vector.tensor_tensor(pair_sums[:], words[:, :, 0:PAIRS], words[:, :, 1:WORDS], ADD)
+            return pair_sums
 
-            for piece in range(LIST // PIECE):
-                columns = slice(
-                    piece * PIECE // OFFSETS_PER_COLUMN, (piece + 1) * PIECE // OFFSETS_PER_COLUMN
-                )
-                picked = work.tile([P, PIECE], F32, name="picked")
-                nc.scalar.activation(picked[:], window[:].indirect(offsets[:, columns]), COPY)
+        def tanh_and_sum(k, block, first, width, pair_sums):
+            pair_tanh = held.tile([P, width // WORDS, PAIRS], F32, name=f"pair_tanh{k}")
+            nc.scalar.activation(pair_tanh[:], pair_sums[:], TANH)
+            sentences = slice(first // WORDS, (first + width) // WORDS)
+            nc.vector.tensor_reduce(sentence_sums[block][:, sentences], pair_tanh[:], INNERMOST, ADD)
+            if first + width == LIST:
+                nc.sync.dma_start(out[block * P : (block + 1) * P, :], sentence_sums[block][:])
 
-                words = picked[:].rearrange("p (b t) -> p b t", t=WORDS)
-                pair_sums = work.tile([P, PIECE_SENTENCES, PAIRS], F32, name="pair_sums")
-                nc.vector.tensor_tensor(
-                    pair_sums[:], words[:, :, 0:PAIRS], words[:, :, 1:WORDS], ADD
-                )
-
-                pair_tanh = work.tile([P, PIECE_SENTENCES, PAIRS], F32, name="pair_tanh")
-                nc.scalar.activation(pair_tanh[:], pair_sums[:], TANH)
-
-                first = piece * PIECE_SENTENCES
-                nc.vector.tensor_reduce(
-                    sentence_sums[:, first : first + PIECE_SENTENCES], pair_tanh[:], INNERMOST, ADD
-                )
-
-            nc.sync.dma_start(out[rows, :], sentence_sums[:])
+        pieces = cut_into_pieces()
+        waiting = None
+        for k, piece in enumerate(pieces):
+            pair_sums = look_up_and_add(k, *piece)
+            if waiting is not None:
+                tanh_and_sum(k - 1, *pieces[k - 1], waiting)
+            waiting = pair_sums
+        tanh_and_sum(len(pieces) - 1, *pieces[-1], waiting)

@@ -15,17 +15,20 @@ PAIRS = WORDS - 1
 LIST = SENTENCES * WORDS
 OFFSETS_PER_COLUMN = 16
 
-WIDTHS = (VOCAB, VOCAB)
-WIDTHS_OF_LAST_BLOCK = (VOCAB, VOCAB // 2, VOCAB // 4, VOCAB // 4)
-assert sum(WIDTHS) == LIST and sum(WIDTHS_OF_LAST_BLOCK) == LIST
+LONG = VOCAB
+SHORT = 4 * WORDS
+CUTS = ((LONG, LONG), (LONG, LONG))
+CUTS_OF_LAST_BLOCK = ((LONG, LONG), (LONG - SHORT, SHORT), (SHORT, SHORT))
+assert sum(width for width, step in CUTS) == LIST
+assert sum(width for width, step in CUTS_OF_LAST_BLOCK) == LIST
 
 
 def cut_into_pieces():
     pieces = []
     for block in range(BLOCKS):
         first = 0
-        for width in WIDTHS_OF_LAST_BLOCK if block == BLOCKS - 1 else WIDTHS:
-            pieces.append((block, first, width))
+        for width, step in CUTS_OF_LAST_BLOCK if block == BLOCKS - 1 else CUTS:
+            pieces.append((block, first, width, step))
             first += width
     return pieces
 
@@ -46,28 +49,33 @@ def tile_bilingual_kernel(tc, table, offs, out):
         nc.vector.memset(dummy[:], 0.0)
         nc.scalar.activation(dummy[:], dummy[:], TANH)
 
-        def look_up_and_add(k, block, first, width):
+        def look_up_and_add(block, first, width):
             columns = slice(first // OFFSETS_PER_COLUMN, (first + width) // OFFSETS_PER_COLUMN)
-            picked = held.tile([P, width], F32, name=f"picked{k}")
+            picked = held.tile([P, width], F32, name=f"picked{block}_{first}")
             nc.scalar.activation(picked[:], windows[block][:].indirect(offsets[:, columns]), COPY)
             words = picked[:].rearrange("p (b t) -> p b t", t=WORDS)
-            pair_sums = held.tile([P, width // WORDS, PAIRS], F32, name=f"pair_sums{k}")
+            pair_sums = held.tile([P, width // WORDS, PAIRS], F32, name=f"pair_sums{block}_{first}")
             nc.vector.tensor_tensor(pair_sums[:], words[:, :, 0:PAIRS], words[:, :, 1:WORDS], ADD)
             return pair_sums
 
-        def tanh_and_sum(k, block, first, width, pair_sums):
-            pair_tanh = held.tile([P, width // WORDS, PAIRS], F32, name=f"pair_tanh{k}")
-            nc.scalar.activation(pair_tanh[:], pair_sums[:], TANH)
-            sentences = slice(first // WORDS, (first + width) // WORDS)
-            nc.vector.tensor_reduce(sentence_sums[block][:, sentences], pair_tanh[:], INNERMOST, ADD)
+        def tanh_and_sum(pair_sums, block, first, width, step):
+            for start in range(0, width, step):
+                inside = slice(start // WORDS, (start + step) // WORDS)
+                pair_tanh = held.tile(
+                    [P, step // WORDS, PAIRS], F32, name=f"pair_tanh{block}_{first + start}"
+                )
+                nc.scalar.activation(pair_tanh[:], pair_sums[:, inside, :], TANH)
+                sentences = slice((first + start) // WORDS, (first + start + step) // WORDS)
+                nc.vector.tensor_reduce(
+                    sentence_sums[block][:, sentences], pair_tanh[:], INNERMOST, ADD
+                )
             if first + width == LIST:
                 nc.sync.dma_start(out[block * P : (block + 1) * P, :], sentence_sums[block][:])
 
-        pieces = cut_into_pieces()
-        waiting = None
-        for k, piece in enumerate(pieces):
-            pair_sums = look_up_and_add(k, *piece)
-            if waiting is not None:
-                tanh_and_sum(k - 1, *pieces[k - 1], waiting)
-            waiting = pair_sums
-        tanh_and_sum(len(pieces) - 1, *pieces[-1], waiting)
+        earlier = None
+        for block, first, width, step in cut_into_pieces():
+            pair_sums = look_up_and_add(block, first, width)
+            if earlier is not None:
+                tanh_and_sum(*earlier)
+            earlier = (pair_sums, block, first, width, step)
+        tanh_and_sum(*earlier)

@@ -39,7 +39,8 @@ def tile_bilingual_kernel(tc, table, offs, out):
         offsets = held.tile([P, LIST // OFFSETS_PER_COLUMN], U16, name="offsets")
         nc.sync.dma_start(offsets[:], offs)
         windows = [held.tile([P, VOCAB], F32, name=f"window{block}") for block in range(BLOCKS)]
-        for block in range(BLOCKS):
+        nc.scalar.dma_start(windows[0][:], table[0:P, :])
+        for block in range(1, BLOCKS):
             nc.sync.dma_start(windows[block][:], table[block * P : (block + 1) * P, :])
         sentence_sums = [
             held.tile([P, SENTENCES], F32, name=f"sentence_sums{block}") for block in range(BLOCKS)

@@ -18,7 +18,7 @@ OFFSETS_PER_COLUMN = 16
 LONG = VOCAB
 SHORT = 4 * WORDS
 CUTS = ((LONG, LONG), (LONG, LONG))
-CUTS_OF_LAST_BLOCK = ((LONG, LONG), (LONG - SHORT, SHORT), (SHORT, SHORT))
+CUTS_OF_LAST_BLOCK = ((LONG, LONG // 2), (LONG - SHORT, SHORT), (SHORT, WORDS))
 assert sum(width for width, step in CUTS) == LIST
 assert sum(width for width, step in CUTS_OF_LAST_BLOCK) == LIST
 
@@ -65,11 +65,19 @@ def tile_bilingual_kernel(tc, table, offs, out):
                 pair_tanh = held.tile(
                     [P, step // WORDS, PAIRS], F32, name=f"pair_tanh{block}_{first + start}"
                 )
-                nc.scalar.activation(pair_tanh[:], pair_sums[:, inside, :], TANH)
                 sentences = slice((first + start) // WORDS, (first + start + step) // WORDS)
-                nc.vector.tensor_reduce(
-                    sentence_sums[block][:, sentences], pair_tanh[:], INNERMOST, ADD
-                )
+                if step == WORDS:
+                    nc.scalar.activation(
+                        pair_tanh[:],
+                        pair_sums[:, inside, :],
+                        TANH,
+                        accum_out=sentence_sums[block][:, sentences],
+                    )
+                else:
+                    nc.scalar.activation(pair_tanh[:], pair_sums[:, inside, :], TANH)
+                    nc.vector.tensor_reduce(
+                        sentence_sums[block][:, sentences], pair_tanh[:], INNERMOST, ADD
+                    )
             if first + width == LIST:
                 nc.sync.dma_start(out[block * P : (block + 1) * P, :], sentence_sums[block][:])
 

@@ -18,7 +18,7 @@ OFFSETS_PER_COLUMN = 16
 LONG = VOCAB
 SHORT = 4 * WORDS
 CUTS = ((LONG, LONG), (LONG, LONG))
-CUTS_OF_LAST_BLOCK = ((LONG, LONG // 2), (LONG - SHORT, SHORT), (SHORT, WORDS))
+CUTS_OF_LAST_BLOCK = ((LONG, LONG // 2), (LONG - SHORT, (LONG - SHORT) // 2), (SHORT, WORDS))
 assert sum(width for width, step in CUTS) == LIST
 assert sum(width for width, step in CUTS_OF_LAST_BLOCK) == LIST
 

import concourse.mybir as mybir

F32 = mybir.dt.float32
U16 = mybir.dt.uint16
COPY = mybir.ActivationFunctionType.Copy
TANH = mybir.ActivationFunctionType.Tanh
ADD = mybir.AluOpType.add
INNERMOST = mybir.AxisListType.X

P = 128
FEATURES, VOCAB = 256, 1024
BLOCKS = FEATURES // P
SENTENCES, WORDS = 32, 64
PAIRS = WORDS - 1
LIST = SENTENCES * WORDS
OFFSETS_PER_COLUMN = 16

LONG = VOCAB
SHORT = 4 * WORDS
CUTS = ((LONG, LONG), (LONG, LONG))
CUTS_OF_LAST_BLOCK = ((LONG, LONG // 2), (LONG - SHORT, (LONG - SHORT) // 2), (SHORT, WORDS))
assert sum(width for width, step in CUTS) == LIST
assert sum(width for width, step in CUTS_OF_LAST_BLOCK) == LIST


def cut_into_pieces():
    pieces = []
    for block in range(BLOCKS):
        first = 0
        for width, step in CUTS_OF_LAST_BLOCK if block == BLOCKS - 1 else CUTS:
            pieces.append((block, first, width, step))
            first += width
    return pieces


def tile_bilingual_kernel(tc, table, offs, out):
    nc = tc.nc
    with tc.tile_pool(name="held", bufs=1) as held:
        offsets = held.tile([P, LIST // OFFSETS_PER_COLUMN], U16, name="offsets")
        nc.sync.dma_start(offsets[:], offs)
        windows = [held.tile([P, VOCAB], F32, name=f"window{block}") for block in range(BLOCKS)]
        nc.scalar.dma_start(windows[0][:], table[0:P, :])
        for block in range(1, BLOCKS):
            nc.sync.dma_start(windows[block][:], table[block * P : (block + 1) * P, :])
        sentence_sums = [
            held.tile([P, SENTENCES], F32, name=f"sentence_sums{block}") for block in range(BLOCKS)
        ]

        dummy = held.tile([P, 1], F32, name="dummy")
        nc.vector.memset(dummy[:], 0.0)
        nc.scalar.activation(dummy[:], dummy[:], TANH)

        def look_up_and_add(block, first, width):
            columns = slice(first // OFFSETS_PER_COLUMN, (first + width) // OFFSETS_PER_COLUMN)
            picked = held.tile([P, width], F32, name=f"picked{block}_{first}")
            nc.scalar.activation(picked[:], windows[block][:].indirect(offsets[:, columns]), COPY)
            words = picked[:].rearrange("p (b t) -> p b t", t=WORDS)
            pair_sums = held.tile([P, width // WORDS, PAIRS], F32, name=f"pair_sums{block}_{first}")
            nc.vector.tensor_tensor(pair_sums[:], words[:, :, 0:PAIRS], words[:, :, 1:WORDS], ADD)
            return pair_sums

        def tanh_and_sum(pair_sums, block, first, width, step):
            for start in range(0, width, step):
                inside = slice(start // WORDS, (start + step) // WORDS)
                pair_tanh = held.tile(
                    [P, step // WORDS, PAIRS], F32, name=f"pair_tanh{block}_{first + start}"
                )
                sentences = slice((first + start) // WORDS, (first + start + step) // WORDS)
                if step == WORDS:
                    nc.scalar.activation(
                        pair_tanh[:],
                        pair_sums[:, inside, :],
                        TANH,
                        accum_out=sentence_sums[block][:, sentences],
                    )
                else:
                    nc.scalar.activation(pair_tanh[:], pair_sums[:, inside, :], TANH)
                    nc.vector.tensor_reduce(
                        sentence_sums[block][:, sentences], pair_tanh[:], INNERMOST, ADD
                    )
            if first + width == LIST:
                nc.sync.dma_start(out[block * P : (block + 1) * P, :], sentence_sums[block][:])

        earlier = None
        for block, first, width, step in cut_into_pieces():
            pair_sums = look_up_and_add(block, first, width)
            if earlier is not None:
                tanh_and_sum(*earlier)
            earlier = (pair_sums, block, first, width, step)
        tanh_and_sum(*earlier)
